import numpy as np
import ml_dtypes

BF16 = ml_dtypes.bfloat16


def bf(x):
    return np.asarray(x, np.float32).astype(BF16)


def f32(x):
    return np.asarray(x, np.float32)


def f64(x):
    return np.asarray(x).astype(np.float64)


def striped(idx):
    return np.tile(idx.reshape(-1, 16).T, (8, 1))


V, S, E, R, N = 1024, 1024, 128, 8, 512


def setup_inputs():
    return {"rel": f32(np.random.choice(R + 1, size=(V, S))), "embed": bf(np.random.standard_normal((V, E))), "src_embed": bf(2.0 * np.random.standard_normal((E, N)) / np.sqrt(E)), "offs": striped(np.random.permutation(np.tile(np.arange(S), 2))[:N])}


def reference(rel, embed, src_embed, offs):
    idx = offs[:16].T.reshape(-1)
    picked = f64(rel)[:, idx]
    base = f64(embed) @ f64(src_embed)
    parts = []
    for r in range(R):
        p = np.exp((picked == r + 1) * base)
        parts.append((f64(embed).T @ p) / p.sum(axis=0, keepdims=True))
    return np.concatenate(parts, axis=0)

@@ -1,0 +1,186 @@
+import concourse.mybir as mybir
+from concourse.masks import make_identity
+
+V, S, E, R, N = 1024, 1024, 128, 8, 512
+P = 128
+VB = V // P
+JC = N // P
+FLOPS = 2 * V * E * N * (R + 1)
+AHEAD = 2
+W = E + 2
+PITCH = 144
+HB = VB // 2
+FIRST = 3
+GROUP = 2
+TILES = max(FIRST, GROUP)
+
+F32 = mybir.dt.float32
+BF16 = mybir.dt.bfloat16
+U16 = mybir.dt.uint16
+ACT = mybir.ActivationFunctionType
+ALU = mybir.AluOpType
+
+
+def tile_graphattention_kernel(tc, rel, embed, src_embed, offs, out):
+    nc = tc.nc
+    with (
+        tc.tile_pool(name="held", bufs=1) as held,
+        tc.tile_pool(name="qpool", bufs=8) as qpool,
+        tc.tile_pool(name="maskpool", bufs=3) as maskpool,
+        tc.tile_pool(name="work", bufs=4) as work,
+        tc.psum_pool(name="setup_ps", bufs=AHEAD) as setup_ps,
+        tc.psum_pool(name="sums_ps", bufs=2 * FIRST) as sums_ps,
+    ):
+        offsets = held.tile([P, N // 16], U16, name="offsets")
+        nc.sync.dma_start(offsets[:], offs)
+        embed_ones = held.tile([P, VB, PITCH], BF16, name="embed_ones")
+        src_sb = held.tile([E, N], BF16, name="src_sb")
+        rel_sb = [held.tile([P, S], F32, name=f"rel{b}") for b in range(VB)]
+        for b in range(HB):
+            nc.sync.dma_start(embed_ones[:, b, 0:E], embed[b * P : (b + 1) * P, :])
+        nc.sync.dma_start(src_sb[:], src_embed)
+        nc.sync.dma_start(rel_sb[0][:], rel[0:P, :])
+        for b in range(HB, VB):
+            nc.sync.dma_start(embed_ones[:, b, 0:E], embed[b * P : (b + 1) * P, :])
+        for b in range(1, VB):
+            nc.sync.dma_start(rel_sb[b][:], rel[b * P : (b + 1) * P, :])
+        nc.gpsimd.memset(embed_ones[:, :, E:W], 1.0)
+
+        warm = held.tile([P, 2], F32, name="warm")
+        nc.vector.memset(warm[:, 0:1], 1.0)
+        nc.scalar.activation(warm[:, 1:2], warm[:, 0:1], ACT.Exp)
+
+        ones = held.tile([P, N], BF16, name="ones")
+        nc.gpsimd.memset(ones[:], 1.0)
+        ident = held.tile([P, P], BF16, name="ident")
+        make_identity(nc, ident[:])
+        ident_f32 = held.tile([P, P], F32, name="ident_f32")
+        make_identity(nc, ident_f32[:])
+
+        expo = {}
+        looked_up = {}
+        gain = held.tile([P, VB, N], BF16, name="gain")
+        picked = held.tile([P, VB, N], BF16, name="picked")
+        finished = []
+        mask_of = {}
+        sums = {}
+
+        def start_block(b):
+            base_ps = setup_ps.tile([P, N], F32, name="base_ps", tag="setup")
+            nc.tensor.matmul(base_ps[:], embT[:, b * P : (b + 1) * P], src_sb[:], start=True, stop=True)
+            looked_up[b] = work.tile([P, N], F32, name="looked_up")
+            nc.scalar.activation(looked_up[b][:], rel_sb[b][:].indirect(offsets[:]), ACT.Copy)
+            expo[b] = work.tile([P, N], F32, name="expo")
+            nc.scalar.activation(expo[b][:], base_ps[:], ACT.Exp)
+
+
+        embT = held.tile([E, V], BF16, name="embT")
+        for h in range(2):
+            embT_ps = sums_ps.tile([E, HB * P], BF16, name="embT_ps", tag="bank")
+            for i in range(HB):
+                nc.tensor.transpose(embT_ps[:, i * P : (i + 1) * P], embed_ones[:, HB * h + i, 0:E], ident[:])
+            nc.vector.tensor_copy(embT[:, HB * h * P : HB * (h + 1) * P], embT_ps[:])
+            if h == 0:
+                for b in range(AHEAD):
+                    start_block(b)
+
+        colsum_ps = sums_ps.tile([P, W], F32, name="colsum_ps", tag="bank")
+        for b in range(VB):
+            nc.tensor.matmul(colsum_ps[:], ones[:, 0:P], embed_ones[:, b, 0:W], start=(b == 0), stop=(b == VB - 1))
+        rounded = held.tile([P, W], BF16, name="rounded")
+        nc.vector.tensor_copy(rounded[:], colsum_ps[:])
+        rest = held.tile([P, W], BF16, name="rest")
+        nc.vector.tensor_sub(rest[:], colsum_ps[:], rounded[:])
+        H = P // 2
+        opening = held.tile([P, 2, W], BF16, name="opening")
+        for i in range(2):
+            nc.vector.tensor_scalar_mul(opening[0:H, i, :], rounded[0:H, :], 1.0 / H)
+            nc.vector.tensor_scalar_mul(opening[H:P, i, :], rest[H:P, :], 1.0 / H)
+
+        def open_banks(r):
+            sums[r] = []
+            for h in range(JC // 2):
+                bank = sums_ps.tile([P, 2, W], F32, name="bank", tag="bank")
+                nc.tensor.matmul(bank[:], ones[:, 0:P], opening[:], start=True, stop=False)
+                sums[r].append(bank)
+
+        def finish_block(b):
+            if b + AHEAD < VB:
+                start_block(b + AHEAD)
+            nc.vector.tensor_copy(picked[:, b, :], looked_up[b][:])
+            nc.vector.tensor_scalar(gain[:, b, :], expo[b][:], -1.0, 3.0e38, op0=ALU.add, op1=ALU.min)
+            finished.append(b)
+
+
+        def make_masks(r0, nr, b0, nb):
+            for b in range(b0, b0 + nb):
+                if b not in finished:
+                    finish_block(b)
+            mask = maskpool.tile([P, TILES, N], BF16, name="mask")
+            for i in range(nr):
+                nc.vector.tensor_single_scalar(
+                    mask[:, i * nb : (i + 1) * nb, :], picked[:, b0 : b0 + nb, :], float(r0 + i + 1), op=ALU.is_equal
+                )
+            mask_of[r0, b0] = mask
+
+        def add_step(r0, nr, b0, nb):
+            q = qpool.tile([P, TILES, N], BF16, name="q")
+            factor = gain[:, b0 : b0 + nb, :]
+            if nr > 1:
+                factor = factor.to_broadcast([P, nr, N])
+            nc.vector.tensor_mul(q[:, 0 : nr * nb, :], mask_of[r0, b0][:, 0 : nr * nb, :], factor)
+            for i in range(nr):
+                for k in range(nb):
+                    for c in range(JC):
+                        nc.tensor.matmul(
+                            sums[r0 + i][c // 2][:, c % 2, :],
+                            q[:, i * nb + k, c * P : (c + 1) * P],
+                            embed_ones[:, b0 + k, 0:W],
+                            start=False,
+                            stop=(b0 + k == VB - 1 and c % 2 == 1),
+                        )
+
+        def divide(r):
+            quot = work.tile([P, JC, E], F32, name="quot")
+            for h in range(JC // 2):
+                recip = work.tile([P, 2, 1], F32, name="recip")
+                if r == R - 1 and h == 1:
+                    nc.vector.reciprocal(recip[:], sums[r][h][:, :, E : E + 1])
+                    for i in range(2):
+                        nc.vector.tensor_scalar_mul(quot[:, 2 * h + i, :], sums[r][h][:, i, 0:E], recip[:, i, :])
+                else:
+                    rsqrt = work.tile([P, 2, 1], F32, name="rsqrt")
+                    nc.scalar.activation(rsqrt[:], sums[r][h][:, :, E : E + 1], ACT.Abs_reciprocal_sqrt)
+                    nc.scalar.activation(recip[:], rsqrt[:], ACT.Square)
+                    for i in range(2):
+                        nc.scalar.activation(
+                            quot[:, 2 * h + i, :], sums[r][h][:, i, 0:E], ACT.Identity, scale=recip[:, i, :]
+                        )
+            return quot
+
+        def turn_back(r, quot):
+            out_ps = setup_ps.tile([E, N], F32, name="out_ps", tag="setup")
+            for c in range(JC):
+                nc.tensor.transpose(out_ps[:, c * P : (c + 1) * P], quot[:, c, :], ident_f32[:])
+            res = work.tile([E, N], F32, name="res")
+            nc.scalar.copy(res[:], out_ps[:])
+            nc.sync.dma_start(out[r * E : (r + 1) * E, :], res[:])
+
+        steps = [(0, FIRST, b, 1) for b in range(VB)]
+        steps += [(r, 1, b0, GROUP) for r in range(FIRST, R) for b0 in range(0, VB, GROUP)]
+        divided = []
+        make_masks(*steps[0])
+        for s, (r0, nr, b0, nb) in enumerate(steps):
+            if s + 1 < len(steps):
+                make_masks(*steps[s + 1])
+            if b0 == 0:
+                for r in range(r0, r0 + nr):
+                    open_banks(r)
+            add_step(r0, nr, b0, nb)
+            if r0 >= FIRST and s % 2 == 1 and divided:
+                turn_back(*divided.pop(0))
+            if b0 + nb == VB:
+                for r in range(r0, r0 + nr):
+                    divided.append((r, divide(r)))
+        for r, quot in divided:
+            turn_back(r, quot)

@@ -50,8 +50,8 @@ def tile_graphattention_kernel(tc, rel, embed, src_embed, offs, out):
         nc.vector.memset(warm[:, 0:1], 1.0)
         nc.scalar.activation(warm[:, 1:2], warm[:, 0:1], ACT.Exp)
 
-        ones = held.tile([P, N], BF16, name="ones")
-        nc.gpsimd.memset(ones[:], 1.0)
+        eighth = held.tile([P, P], BF16, name="eighth")
+        nc.gpsimd.memset(eighth[:], 0.125)
         ident = held.tile([P, P], BF16, name="ident")
         make_identity(nc, ident[:])
         ident_f32 = held.tile([P, P], F32, name="ident_f32")
@@ -63,6 +63,7 @@ def tile_graphattention_kernel(tc, rel, embed, src_embed, offs, out):
         picked = held.tile([P, VB, N], BF16, name="picked")
         finished = []
         mask_of = {}
+        quot = held.tile([P, R, JC, E], F32, name="quot")
         sums = {}
 
         def start_block(b):
@@ -70,7 +71,7 @@ def tile_graphattention_kernel(tc, rel, embed, src_embed, offs, out):
             nc.tensor.matmul(base_ps[:], embT[:, b * P : (b + 1) * P], src_sb[:], start=True, stop=True)
             looked_up[b] = work.tile([P, N], F32, name="looked_up")
             nc.scalar.activation(looked_up[b][:], rel_sb[b][:].indirect(offsets[:]), ACT.Copy)
-            expo[b] = work.tile([P, N], F32, name="expo")
+            expo[b] = work.tile([P, N], BF16, name="expo")
             nc.scalar.activation(expo[b][:], base_ps[:], ACT.Exp)
 
 
@@ -86,22 +87,22 @@ def tile_graphattention_kernel(tc, rel, embed, src_embed, offs, out):
 
         colsum_ps = sums_ps.tile([P, W], F32, name="colsum_ps", tag="bank")
         for b in range(VB):
-            nc.tensor.matmul(colsum_ps[:], ones[:, 0:P], embed_ones[:, b, 0:W], start=(b == 0), stop=(b == VB - 1))
-        rounded = held.tile([P, W], BF16, name="rounded")
-        nc.vector.tensor_copy(rounded[:], colsum_ps[:])
-        rest = held.tile([P, W], BF16, name="rest")
-        nc.vector.tensor_sub(rest[:], colsum_ps[:], rounded[:])
-        H = P // 2
-        opening = held.tile([P, 2, W], BF16, name="opening")
-        for i in range(2):
-            nc.vector.tensor_scalar_mul(opening[0:H, i, :], rounded[0:H, :], 1.0 / H)
-            nc.vector.tensor_scalar_mul(opening[H:P, i, :], rest[H:P, :], 1.0 / H)
+            nc.tensor.matmul(colsum_ps[:], eighth[:], embed_ones[:, b, 0:W], start=(b == 0), stop=(b == VB - 1))
+        sum_row = held.tile([P, W], BF16, name="sum_row")
+        nc.vector.tensor_copy(sum_row[:], colsum_ps[:])
+        rest = slice(P // 2, P)
+        nc.vector.tensor_sub(sum_row[rest, :], colsum_ps[rest, :], sum_row[rest, :])
 
         def open_banks(r):
             sums[r] = []
             for h in range(JC // 2):
-                bank = sums_ps.tile([P, 2, W], F32, name="bank", tag="bank")
-                nc.tensor.matmul(bank[:], ones[:, 0:P], opening[:], start=True, stop=False)
+                if r == FIRST:
+                    bank = setup_ps.tile([P, 2, W], F32, name="late_bank", tag="setup")
+                else:
+                    bank = sums_ps.tile([P, 2, W], F32, name="bank", tag="bank")
+                nc.tensor.matmul(
+                    bank[:], eighth[:], sum_row[:].unsqueeze(1).to_broadcast([P, 2, W]), start=True, stop=False
+                )
                 sums[r].append(bank)
 
         def finish_block(b):
@@ -112,75 +113,74 @@ def tile_graphattention_kernel(tc, rel, embed, src_embed, offs, out):
             finished.append(b)
 
 
-        def make_masks(r0, nr, b0, nb):
+        def make_masks(r0, nr, b0, nb, c0, nc_):
             for b in range(b0, b0 + nb):
                 if b not in finished:
                     finish_block(b)
-            mask = maskpool.tile([P, TILES, N], BF16, name="mask")
+            tokens = slice(c0 * P, (c0 + nc_) * P)
+            mask = maskpool.tile([P, nr * nb, nc_ * P], BF16, name="mask")
             for i in range(nr):
                 nc.vector.tensor_single_scalar(
-                    mask[:, i * nb : (i + 1) * nb, :], picked[:, b0 : b0 + nb, :], float(r0 + i + 1), op=ALU.is_equal
+                    mask[:, i * nb : (i + 1) * nb, :], picked[:, b0 : b0 + nb, tokens], float(r0 + i + 1), op=ALU.is_equal
                 )
-            mask_of[r0, b0] = mask
+            mask_of[r0, b0, c0] = mask
 
-        def add_step(r0, nr, b0, nb):
-            q = qpool.tile([P, TILES, N], BF16, name="q")
-            factor = gain[:, b0 : b0 + nb, :]
+        def add_step(r0, nr, b0, nb, c0, nc_):
+            q = qpool.tile([P, nr * nb, nc_ * P], BF16, name="q")
+            factor = gain[:, b0 : b0 + nb, c0 * P : (c0 + nc_) * P]
             if nr > 1:
                 factor = factor.to_broadcast([P, nr, N])
-            nc.vector.tensor_mul(q[:, 0 : nr * nb, :], mask_of[r0, b0][:, 0 : nr * nb, :], factor)
+            nc.vector.tensor_mul(q[:], mask_of[r0, b0, c0][:], factor)
             for i in range(nr):
                 for k in range(nb):
-                    for c in range(JC):
+                    for c in range(c0, c0 + nc_):
                         nc.tensor.matmul(
                             sums[r0 + i][c // 2][:, c % 2, :],
-                            q[:, i * nb + k, c * P : (c + 1) * P],
+                            q[:, i * nb + k, (c - c0) * P : (c - c0 + 1) * P],
                             embed_ones[:, b0 + k, 0:W],
                             start=False,
                             stop=(b0 + k == VB - 1 and c % 2 == 1),
                         )
 
-        def divide(r):
-            quot = work.tile([P, JC, E], F32, name="quot")
-            for h in range(JC // 2):
-                recip = work.tile([P, 2, 1], F32, name="recip")
-                if r == R - 1 and h == 1:
-                    nc.vector.reciprocal(recip[:], sums[r][h][:, :, E : E + 1])
-                    for i in range(2):
-                        nc.vector.tensor_scalar_mul(quot[:, 2 * h + i, :], sums[r][h][:, i, 0:E], recip[:, i, :])
-                else:
-                    rsqrt = work.tile([P, 2, 1], F32, name="rsqrt")
-                    nc.scalar.activation(rsqrt[:], sums[r][h][:, :, E : E + 1], ACT.Abs_reciprocal_sqrt)
-                    nc.scalar.activation(recip[:], rsqrt[:], ACT.Square)
-                    for i in range(2):
-                        nc.scalar.activation(
-                            quot[:, 2 * h + i, :], sums[r][h][:, i, 0:E], ACT.Identity, scale=recip[:, i, :]
-                        )
-            return quot
+        def divide(r, h):
+            bank = sums[r][h]
+            recip = work.tile([P, 2, 1], F32, name="recip")
+            if r == R - 1 and h == 1:
+                nc.vector.reciprocal(recip[:], bank[:, :, E : E + 1])
+                nc.vector.tensor_mul(quot[:, r, 2:4, :], bank[:, :, 0:E], recip[:].to_broadcast([P, 2, E]))
+            else:
+                rsqrt = work.tile([P, 2, 1], F32, name="rsqrt")
+                nc.scalar.activation(rsqrt[:], bank[:, :, E : E + 1], ACT.Abs_reciprocal_sqrt)
+                nc.scalar.activation(recip[:], rsqrt[:], ACT.Square)
+                for i in range(2):
+                    nc.scalar.activation(quot[:, r, 2 * h + i, :], bank[:, i, 0:E], ACT.Identity, scale=recip[:, i, :])
 
-        def turn_back(r, quot):
-            out_ps = setup_ps.tile([E, N], F32, name="out_ps", tag="setup")
-            for c in range(JC):
-                nc.tensor.transpose(out_ps[:, c * P : (c + 1) * P], quot[:, c, :], ident_f32[:])
-            res = work.tile([E, N], F32, name="res")
+        def turn_back(r, c0, n):
+            out_ps = sums_ps.tile([E, n * P], F32, name="out_ps", tag="bank")
+            for c in range(n):
+                nc.tensor.transpose(out_ps[:, c * P : (c + 1) * P], quot[:, r, c0 + c, :], ident_f32[:])
+            res = work.tile([E, n * P], F32, name="res")
             nc.scalar.copy(res[:], out_ps[:])
-            nc.sync.dma_start(out[r * E : (r + 1) * E, :], res[:])
+            nc.sync.dma_start(out[r * E : (r + 1) * E, c0 * P : (c0 + n) * P], res[:])
 
-        steps = [(0, FIRST, b, 1) for b in range(VB)]
-        steps += [(r, 1, b0, GROUP) for r in range(FIRST, R) for b0 in range(0, VB, GROUP)]
+        steps = [(0, FIRST, b, 1, 0, JC) for b in range(VB)]
+        steps += [(r, 1, b0, GROUP, 0, JC) for r in range(FIRST, R - 1) for b0 in range(0, VB, GROUP)]
+        steps += [(R - 1, 1, b0, 2 * GROUP, c0, 2) for c0 in (0, 2) for b0 in range(0, VB, 2 * GROUP)]
         divided = []
         make_masks(*steps[0])
-        for s, (r0, nr, b0, nb) in enumerate(steps):
+        for s, (r0, nr, b0, nb, c0, nc_) in enumerate(steps):
             if s + 1 < len(steps):
                 make_masks(*steps[s + 1])
-            if b0 == 0:
+            if b0 == 0 and c0 == 0:
                 for r in range(r0, r0 + nr):
                     open_banks(r)
-            add_step(r0, nr, b0, nb)
+            add_step(r0, nr, b0, nb, c0, nc_)
             if r0 >= FIRST and s % 2 == 1 and divided:
                 turn_back(*divided.pop(0))
             if b0 + nb == VB:
                 for r in range(r0, r0 + nr):
-                    divided.append((r, divide(r)))
-        for r, quot in divided:
-            turn_back(r, quot)
+                    for h in range(c0 // 2, (c0 + nc_) // 2):
+                        divide(r, h)
+                    divided.append((r, c0, nc_))
+        for part in divided:
+            turn_back(*part)

@@ -64,6 +64,8 @@ def tile_graphattention_kernel(tc, rel, embed, src_embed, offs, out):
         finished = []
         mask_of = {}
         quot = held.tile([P, R, JC, E], F32, name="quot")
+        last_mask = held.tile([P, VB // 2, N], BF16, name="last_mask")
+        less_seven = held.tile([P, 1], F32, name="less_seven")
         sums = {}
 
         def start_block(b):
@@ -108,9 +110,18 @@ def tile_graphattention_kernel(tc, rel, embed, src_embed, offs, out):
         def finish_block(b):
             if b + AHEAD < VB:
                 start_block(b + AHEAD)
-            nc.vector.tensor_copy(picked[:, b, :], looked_up[b][:])
+            if b < VB - 1:
+                nc.vector.tensor_copy(picked[:, b, :], looked_up[b][:])
+            else:
+                nc.scalar.copy(picked[:, b, :], looked_up[b][:])
             nc.vector.tensor_scalar(gain[:, b, :], expo[b][:], -1.0, 3.0e38, op0=ALU.add, op1=ALU.min)
             finished.append(b)
+            if b == VB - 1:
+                nc.vector.tensor_scalar(
+                    less_seven[:], picked[:, b, 0:1], 0.0, -float(R - 1), op0=ALU.mult, op1=ALU.add
+                )
+                for k in range(VB // 2):
+                    nc.scalar.activation(last_mask[:, k, :], picked[:, VB // 2 + k, :], ACT.Relu, bias=less_seven[:])
 
 
         def make_masks(r0, nr, b0, nb, c0, nc_):
@@ -118,19 +129,22 @@ def tile_graphattention_kernel(tc, rel, embed, src_embed, offs, out):
                 if b not in finished:
                     finish_block(b)
             tokens = slice(c0 * P, (c0 + nc_) * P)
+            if r0 == R - 1 and b0 >= VB // 2:
+                mask_of[r0, b0, c0] = last_mask[:, b0 - VB // 2 : b0 - VB // 2 + nb, tokens]
+                return
             mask = maskpool.tile([P, nr * nb, nc_ * P], BF16, name="mask")
             for i in range(nr):
                 nc.vector.tensor_single_scalar(
                     mask[:, i * nb : (i + 1) * nb, :], picked[:, b0 : b0 + nb, tokens], float(r0 + i + 1), op=ALU.is_equal
                 )
-            mask_of[r0, b0, c0] = mask
+            mask_of[r0, b0, c0] = mask[:]
 
         def add_step(r0, nr, b0, nb, c0, nc_):
             q = qpool.tile([P, nr * nb, nc_ * P], BF16, name="q")
             factor = gain[:, b0 : b0 + nb, c0 * P : (c0 + nc_) * P]
             if nr > 1:
                 factor = factor.to_broadcast([P, nr, N])
-            nc.vector.tensor_mul(q[:], mask_of[r0, b0, c0][:], factor)
+            nc.vector.tensor_mul(q[:], mask_of[r0, b0, c0], factor)
             for i in range(nr):
                 for k in range(nb):
                     for c in range(c0, c0 + nc_):

@@ -51,7 +51,6 @@ def tile_graphattention_kernel(tc, rel, embed, src_embed, offs, out):
         nc.scalar.activation(warm[:, 1:2], warm[:, 0:1], ACT.Exp)
 
         eighth = held.tile([P, P], BF16, name="eighth")
-        nc.gpsimd.memset(eighth[:], 0.125)
         ident = held.tile([P, P], BF16, name="ident")
         make_identity(nc, ident[:])
         ident_f32 = held.tile([P, P], F32, name="ident_f32")
@@ -72,20 +71,23 @@ def tile_graphattention_kernel(tc, rel, embed, src_embed, offs, out):
             base_ps = setup_ps.tile([P, N], F32, name="base_ps", tag="setup")
             nc.tensor.matmul(base_ps[:], embT[:, b * P : (b + 1) * P], src_sb[:], start=True, stop=True)
             looked_up[b] = work.tile([P, N], F32, name="looked_up")
+            nc.vector.tensor_copy(looked_up[b][:, 0:1], embT[:, 0:1])
             nc.scalar.activation(looked_up[b][:], rel_sb[b][:].indirect(offsets[:]), ACT.Copy)
             expo[b] = work.tile([P, N], BF16, name="expo")
             nc.scalar.activation(expo[b][:], base_ps[:], ACT.Exp)
 
 
         embT = held.tile([E, V], BF16, name="embT")
+        embT_ps = sums_ps.tile([E, HB * P], BF16, name="embT_ps", tag="bank")
         for h in range(2):
-            embT_ps = sums_ps.tile([E, HB * P], BF16, name="embT_ps", tag="bank")
             for i in range(HB):
                 nc.tensor.transpose(embT_ps[:, i * P : (i + 1) * P], embed_ones[:, HB * h + i, 0:E], ident[:])
             nc.vector.tensor_copy(embT[:, HB * h * P : HB * (h + 1) * P], embT_ps[:])
             if h == 0:
                 for b in range(AHEAD):
                     start_block(b)
+
+        nc.vector.tensor_scalar(eighth[:], embT[:, V - P : V], 0.0, 0.125, op0=ALU.mult, op1=ALU.add)
 
         colsum_ps = sums_ps.tile([P, W], F32, name="colsum_ps", tag="bank")
         for b in range(VB):

@@ -9,10 +9,14 @@ FLOPS = 2 * V * E * N * (R + 1)
 AHEAD = 2
 W = E + 2
 PITCH = 144
-HB = VB // 2
+TURN = 4
 FIRST = 3
+LATER = (3, 4, 7, 5, 6)
+LAST = LATER[-1]
+BANKS = ((0, 2), (2, 2))
+LAST_BANKS = ((0, 2), (2, 1), (3, 1))
+LAST_GROUPS = (4, 8, 4)
 GROUP = 2
-TILES = max(FIRST, GROUP)
 
 F32 = mybir.dt.float32
 BF16 = mybir.dt.bfloat16
@@ -36,11 +40,11 @@ def tile_graphattention_kernel(tc, rel, embed, src_embed, offs, out):
         embed_ones = held.tile([P, VB, PITCH], BF16, name="embed_ones")
         src_sb = held.tile([E, N], BF16, name="src_sb")
         rel_sb = [held.tile([P, S], F32, name=f"rel{b}") for b in range(VB)]
-        for b in range(HB):
+        for b in range(TURN):
             nc.sync.dma_start(embed_ones[:, b, 0:E], embed[b * P : (b + 1) * P, :])
         nc.sync.dma_start(src_sb[:], src_embed)
         nc.sync.dma_start(rel_sb[0][:], rel[0:P, :])
-        for b in range(HB, VB):
+        for b in range(TURN, VB):
             nc.sync.dma_start(embed_ones[:, b, 0:E], embed[b * P : (b + 1) * P, :])
         for b in range(1, VB):
             nc.sync.dma_start(rel_sb[b][:], rel[b * P : (b + 1) * P, :])
@@ -50,64 +54,64 @@ def tile_graphattention_kernel(tc, rel, embed, src_embed, offs, out):
         nc.vector.memset(warm[:, 0:1], 1.0)
         nc.scalar.activation(warm[:, 1:2], warm[:, 0:1], ACT.Exp)
 
-        eighth = held.tile([P, P], BF16, name="eighth")
         ident = held.tile([P, P], BF16, name="ident")
         make_identity(nc, ident[:])
         ident_f32 = held.tile([P, P], F32, name="ident_f32")
         make_identity(nc, ident_f32[:])
+        less_seven = held.tile([P, 1], F32, name="less_seven")
+        nc.gpsimd.memset(less_seven[:], -float(R - 1))
 
-        expo = {}
-        looked_up = {}
-        gain = held.tile([P, VB, N], BF16, name="gain")
+        looked_up = [held.tile([P, N], F32, name=f"looked_up{b}") for b in range(VB)]
         picked = held.tile([P, VB, N], BF16, name="picked")
+        expo = {}
+        gain = held.tile([P, VB, N], BF16, name="gain")
+        embT = held.tile([E, V], BF16, name="embT")
+        eighth = held.tile([P, P], BF16, name="eighth")
+        sum_row = held.tile([P, W], BF16, name="sum_row")
+        relu_mask = held.tile([P, VB // 2, N], BF16, name="relu_mask")
+        quot = held.tile([P, R, JC, E], F32, name="quot")
         finished = []
         mask_of = {}
-        quot = held.tile([P, R, JC, E], F32, name="quot")
-        last_mask = held.tile([P, VB // 2, N], BF16, name="last_mask")
-        less_seven = held.tile([P, 1], F32, name="less_seven")
-        sums = {}
+        place = {}
 
         def start_block(b):
             base_ps = setup_ps.tile([P, N], F32, name="base_ps", tag="setup")
             nc.tensor.matmul(base_ps[:], embT[:, b * P : (b + 1) * P], src_sb[:], start=True, stop=True)
-            looked_up[b] = work.tile([P, N], F32, name="looked_up")
             nc.vector.tensor_copy(looked_up[b][:, 0:1], embT[:, 0:1])
             nc.scalar.activation(looked_up[b][:], rel_sb[b][:].indirect(offsets[:]), ACT.Copy)
             expo[b] = work.tile([P, N], BF16, name="expo")
             nc.scalar.activation(expo[b][:], base_ps[:], ACT.Exp)
 
 
-        embT = held.tile([E, V], BF16, name="embT")
-        embT_ps = sums_ps.tile([E, HB * P], BF16, name="embT_ps", tag="bank")
-        for h in range(2):
-            for i in range(HB):
-                nc.tensor.transpose(embT_ps[:, i * P : (i + 1) * P], embed_ones[:, HB * h + i, 0:E], ident[:])
-            nc.vector.tensor_copy(embT[:, HB * h * P : HB * (h + 1) * P], embT_ps[:])
-            if h == 0:
+        embT_ps = sums_ps.tile([E, TURN * P], BF16, name="embT_ps", tag="bank")
+        for b0 in range(0, VB, TURN):
+            for k in range(TURN):
+                nc.tensor.transpose(embT_ps[:, k * P : (k + 1) * P], embed_ones[:, b0 + k, 0:E], ident[:])
+            nc.vector.tensor_copy(embT[:, b0 * P : (b0 + TURN) * P], embT_ps[:])
+            if b0 == 0:
                 for b in range(AHEAD):
                     start_block(b)
 
         nc.vector.tensor_scalar(eighth[:], embT[:, V - P : V], 0.0, 0.125, op0=ALU.mult, op1=ALU.add)
-
         colsum_ps = sums_ps.tile([P, W], F32, name="colsum_ps", tag="bank")
         for b in range(VB):
             nc.tensor.matmul(colsum_ps[:], eighth[:], embed_ones[:, b, 0:W], start=(b == 0), stop=(b == VB - 1))
-        sum_row = held.tile([P, W], BF16, name="sum_row")
         nc.vector.tensor_copy(sum_row[:], colsum_ps[:])
         rest = slice(P // 2, P)
         nc.vector.tensor_sub(sum_row[rest, :], colsum_ps[rest, :], sum_row[rest, :])
 
-        def open_banks(r):
-            sums[r] = []
-            for h in range(JC // 2):
-                if r == FIRST:
-                    bank = setup_ps.tile([P, 2, W], F32, name="late_bank", tag="setup")
-                else:
-                    bank = sums_ps.tile([P, 2, W], F32, name="bank", tag="bank")
-                nc.tensor.matmul(
-                    bank[:], eighth[:], sum_row[:].unsqueeze(1).to_broadcast([P, 2, W]), start=True, stop=False
-                )
-                sums[r].append(bank)
+        def banks_in(r, c0, n):
+            return [(c, m) for c, m in (LAST_BANKS if r == LAST else BANKS) if c0 <= c and c + m <= c0 + n]
+
+        def open_bank(r, c0, n):
+            if r == LATER[0]:
+                bank = setup_ps.tile([P, n, W], F32, name="late_bank", tag="setup")
+            else:
+                bank = sums_ps.tile([P, n, W], F32, name="bank", tag="bank")
+            row_of_each_chunk = sum_row[:].unsqueeze(1).to_broadcast([P, n, W])
+            nc.tensor.matmul(bank[:], eighth[:], row_of_each_chunk, start=True, stop=False)
+            for i in range(n):
+                place[r, c0 + i] = bank, i
 
         def finish_block(b):
             if b + AHEAD < VB:
@@ -119,84 +123,84 @@ def tile_graphattention_kernel(tc, rel, embed, src_embed, offs, out):
             nc.vector.tensor_scalar(gain[:, b, :], expo[b][:], -1.0, 3.0e38, op0=ALU.add, op1=ALU.min)
             finished.append(b)
             if b == VB - 1:
-                nc.vector.tensor_scalar(
-                    less_seven[:], picked[:, b, 0:1], 0.0, -float(R - 1), op0=ALU.mult, op1=ALU.add
-                )
-                for k in range(VB // 2):
-                    nc.scalar.activation(last_mask[:, k, :], picked[:, VB // 2 + k, :], ACT.Relu, bias=less_seven[:])
+                nc.scalar.activation(relu_mask[:], picked[:, VB // 2 : VB, :], ACT.Relu, bias=less_seven[:])
 
 
-        def make_masks(r0, nr, b0, nb, c0, nc_):
+        def make_masks(r0, nr, b0, nb, c0, n):
             for b in range(b0, b0 + nb):
                 if b not in finished:
                     finish_block(b)
-            tokens = slice(c0 * P, (c0 + nc_) * P)
+            tokens = slice(c0 * P, (c0 + n) * P)
             if r0 == R - 1 and b0 >= VB // 2:
-                mask_of[r0, b0, c0] = last_mask[:, b0 - VB // 2 : b0 - VB // 2 + nb, tokens]
+                mask_of[r0, b0, c0] = relu_mask[:, b0 - VB // 2 : b0 - VB // 2 + nb, tokens]
                 return
-            mask = maskpool.tile([P, nr * nb, nc_ * P], BF16, name="mask")
+            mask = maskpool.tile([P, nr * nb, n * P], BF16, name="mask")
             for i in range(nr):
                 nc.vector.tensor_single_scalar(
                     mask[:, i * nb : (i + 1) * nb, :], picked[:, b0 : b0 + nb, tokens], float(r0 + i + 1), op=ALU.is_equal
                 )
             mask_of[r0, b0, c0] = mask[:]
 
-        def add_step(r0, nr, b0, nb, c0, nc_):
-            q = qpool.tile([P, nr * nb, nc_ * P], BF16, name="q")
-            factor = gain[:, b0 : b0 + nb, c0 * P : (c0 + nc_) * P]
+        def add_step(r0, nr, b0, nb, c0, n):
+            q = qpool.tile([P, nr * nb, n * P], BF16, name="q")
+            factor = gain[:, b0 : b0 + nb, c0 * P : (c0 + n) * P]
             if nr > 1:
-                factor = factor.to_broadcast([P, nr, N])
+                factor = factor.to_broadcast([P, nr, n * P])
             nc.vector.tensor_mul(q[:], mask_of[r0, b0, c0], factor)
             for i in range(nr):
                 for k in range(nb):
-                    for c in range(c0, c0 + nc_):
+                    for c in range(c0, c0 + n):
+                        bank, slot = place[r0 + i, c]
                         nc.tensor.matmul(
-                            sums[r0 + i][c // 2][:, c % 2, :],
+                            bank[:, slot, :],
                             q[:, i * nb + k, (c - c0) * P : (c - c0 + 1) * P],
                             embed_ones[:, b0 + k, 0:W],
                             start=False,
-                            stop=(b0 + k == VB - 1 and c % 2 == 1),
+                            stop=(b0 + k == VB - 1 and slot == bank.shape[1] - 1),
                         )
 
-        def divide(r, h):
-            bank = sums[r][h]
-            recip = work.tile([P, 2, 1], F32, name="recip")
-            if r == R - 1 and h == 1:
+        def divide(r, c0, n):
+            bank, _ = place[r, c0]
+            recip = work.tile([P, n, 1], F32, name="recip")
+            if r == LAST and c0 + n == JC:
                 nc.vector.reciprocal(recip[:], bank[:, :, E : E + 1])
-                nc.vector.tensor_mul(quot[:, r, 2:4, :], bank[:, :, 0:E], recip[:].to_broadcast([P, 2, E]))
-            else:
-                rsqrt = work.tile([P, 2, 1], F32, name="rsqrt")
-                nc.scalar.activation(rsqrt[:], bank[:, :, E : E + 1], ACT.Abs_reciprocal_sqrt)
-                nc.scalar.activation(recip[:], rsqrt[:], ACT.Square)
-                for i in range(2):
-                    nc.scalar.activation(quot[:, r, 2 * h + i, :], bank[:, i, 0:E], ACT.Identity, scale=recip[:, i, :])
+                nc.vector.tensor_mul(quot[:, r, c0 : c0 + n, :], bank[:, :, 0:E], recip[:].to_broadcast([P, n, E]))
+                return
+            rsqrt = work.tile([P, n, 1], F32, name="rsqrt")
+            nc.scalar.activation(rsqrt[:], bank[:, :, E : E + 1], ACT.Abs_reciprocal_sqrt)
+            nc.scalar.activation(recip[:], rsqrt[:], ACT.Square)
+            for i in range(n):
+                nc.scalar.activation(quot[:, r, c0 + i, :], bank[:, i, 0:E], ACT.Identity, scale=recip[:, i, :])
 
         def turn_back(r, c0, n):
             out_ps = sums_ps.tile([E, n * P], F32, name="out_ps", tag="bank")
-            for c in range(n):
-                nc.tensor.transpose(out_ps[:, c * P : (c + 1) * P], quot[:, r, c0 + c, :], ident_f32[:])
+            for i in range(n):
+                nc.tensor.transpose(out_ps[:, i * P : (i + 1) * P], quot[:, r, c0 + i, :], ident_f32[:])
             res = work.tile([E, n * P], F32, name="res")
             nc.scalar.copy(res[:], out_ps[:])
             nc.sync.dma_start(out[r * E : (r + 1) * E, c0 * P : (c0 + n) * P], res[:])
 
         steps = [(0, FIRST, b, 1, 0, JC) for b in range(VB)]
-        steps += [(r, 1, b0, GROUP, 0, JC) for r in range(FIRST, R - 1) for b0 in range(0, VB, GROUP)]
-        steps += [(R - 1, 1, b0, 2 * GROUP, c0, 2) for c0 in (0, 2) for b0 in range(0, VB, 2 * GROUP)]
+        steps += [(r, 1, b0, GROUP, 0, JC) for r in LATER[:-1] for b0 in range(0, VB, GROUP)]
+        steps += [
+            (LAST, 1, b0, group, c0, n) for (c0, n), group in zip(LAST_BANKS, LAST_GROUPS) for b0 in range(0, VB, group)
+        ]
         divided = []
         make_masks(*steps[0])
-        for s, (r0, nr, b0, nb, c0, nc_) in enumerate(steps):
+        for s, (r0, nr, b0, nb, c0, n) in enumerate(steps):
             if s + 1 < len(steps):
                 make_masks(*steps[s + 1])
-            if b0 == 0 and c0 == 0:
-                for r in range(r0, r0 + nr):
-                    open_banks(r)
-            add_step(r0, nr, b0, nb, c0, nc_)
-            if r0 >= FIRST and s % 2 == 1 and divided:
+            for r in range(r0, r0 + nr):
+                if b0 == 0:
+                    for bank in banks_in(r, c0, n):
+                        open_bank(r, *bank)
+            add_step(r0, nr, b0, nb, c0, n)
+            if s > VB + AHEAD and s % 2 == 1 and divided and divided[0][0] != LAST:
                 turn_back(*divided.pop(0))
             if b0 + nb == VB:
                 for r in range(r0, r0 + nr):
-                    for h in range(c0 // 2, (c0 + nc_) // 2):
-                        divide(r, h)
-                    divided.append((r, c0, nc_))
+                    for bank in banks_in(r, c0, n):
+                        divide(r, *bank)
+                    divided.append((r, c0, n))
         for part in divided:
             turn_back(*part)

@@ -59,9 +59,8 @@ def tile_graphattention_kernel(tc, rel, embed, src_embed, offs, out):
         ident_f32 = held.tile([P, P], F32, name="ident_f32")
         make_identity(nc, ident_f32[:])
         less_seven = held.tile([P, 1], F32, name="less_seven")
-        nc.gpsimd.memset(less_seven[:], -float(R - 1))
 
-        looked_up = [held.tile([P, N], F32, name=f"looked_up{b}") for b in range(VB)]
+        looked_up = {}
         picked = held.tile([P, VB, N], BF16, name="picked")
         expo = {}
         gain = held.tile([P, VB, N], BF16, name="gain")
@@ -77,6 +76,7 @@ def tile_graphattention_kernel(tc, rel, embed, src_embed, offs, out):
         def start_block(b):
             base_ps = setup_ps.tile([P, N], F32, name="base_ps", tag="setup")
             nc.tensor.matmul(base_ps[:], embT[:, b * P : (b + 1) * P], src_sb[:], start=True, stop=True)
+            looked_up[b] = work.tile([P, N], F32, name="looked_up")
             nc.vector.tensor_copy(looked_up[b][:, 0:1], embT[:, 0:1])
             nc.scalar.activation(looked_up[b][:], rel_sb[b][:].indirect(offsets[:]), ACT.Copy)
             expo[b] = work.tile([P, N], BF16, name="expo")
@@ -123,7 +123,11 @@ def tile_graphattention_kernel(tc, rel, embed, src_embed, offs, out):
             nc.vector.tensor_scalar(gain[:, b, :], expo[b][:], -1.0, 3.0e38, op0=ALU.add, op1=ALU.min)
             finished.append(b)
             if b == VB - 1:
-                nc.scalar.activation(relu_mask[:], picked[:, VB // 2 : VB, :], ACT.Relu, bias=less_seven[:])
+                nc.vector.tensor_scalar(
+                    less_seven[:], picked[:, b, 0:1], 0.0, -float(R - 1), op0=ALU.mult, op1=ALU.add
+                )
+                for k in range(VB // 2):
+                    nc.scalar.activation(relu_mask[:, k, :], picked[:, VB // 2 + k, :], ACT.Relu, bias=less_seven[:])
 
 
         def make_masks(r0, nr, b0, nb, c0, n):

@@ -59,6 +59,7 @@ def tile_graphattention_kernel(tc, rel, embed, src_embed, offs, out):
         ident_f32 = held.tile([P, P], F32, name="ident_f32")
         make_identity(nc, ident_f32[:])
         less_seven = held.tile([P, 1], F32, name="less_seven")
+        nc.gpsimd.memset(less_seven[:], -float(R - 1))
 
         looked_up = {}
         picked = held.tile([P, VB, N], BF16, name="picked")
@@ -123,11 +124,7 @@ def tile_graphattention_kernel(tc, rel, embed, src_embed, offs, out):
             nc.vector.tensor_scalar(gain[:, b, :], expo[b][:], -1.0, 3.0e38, op0=ALU.add, op1=ALU.min)
             finished.append(b)
             if b == VB - 1:
-                nc.vector.tensor_scalar(
-                    less_seven[:], picked[:, b, 0:1], 0.0, -float(R - 1), op0=ALU.mult, op1=ALU.add
-                )
-                for k in range(VB // 2):
-                    nc.scalar.activation(relu_mask[:, k, :], picked[:, VB // 2 + k, :], ACT.Relu, bias=less_seven[:])
+                nc.scalar.activation(relu_mask[:], picked[:, VB // 2 : VB, :], ACT.Relu, bias=less_seven[:])
 
 
         def make_masks(r0, nr, b0, nb, c0, n):
@@ -181,7 +178,10 @@ def tile_graphattention_kernel(tc, rel, embed, src_embed, offs, out):
             for i in range(n):
                 nc.tensor.transpose(out_ps[:, i * P : (i + 1) * P], quot[:, r, c0 + i, :], ident_f32[:])
             res = work.tile([E, n * P], F32, name="res")
-            nc.scalar.copy(res[:], out_ps[:])
+            if r == LAST and c0 + n == JC:
+                nc.vector.tensor_copy(res[:], out_ps[:])
+            else:
+                nc.scalar.copy(res[:], out_ps[:])
             nc.sync.dma_start(out[r * E : (r + 1) * E, c0 * P : (c0 + n) * P], res[:])
 
         steps = [(0, FIRST, b, 1, 0, JC) for b in range(VB)]
@@ -199,7 +199,7 @@ def tile_graphattention_kernel(tc, rel, embed, src_embed, offs, out):
                     for bank in banks_in(r, c0, n):
                         open_bank(r, *bank)
             add_step(r0, nr, b0, nb, c0, n)
-            if s > VB + AHEAD and s % 2 == 1 and divided and divided[0][0] != LAST:
+            if s > VB + AHEAD and s % 2 == 1 and divided and r0 != LAST:
                 turn_back(*divided.pop(0))
             if b0 + nb == VB:
                 for r in range(r0, r0 + nr):

@@ -9,7 +9,7 @@ FLOPS = 2 * V * E * N * (R + 1)
 AHEAD = 2
 W = E + 2
 PITCH = 144
-TURN = 4
+TURNS = ((0, 2), (2, 2), (4, 4))
 FIRST = 3
 LATER = (3, 4, 7, 5, 6)
 LAST = LATER[-1]
@@ -40,14 +40,18 @@ def tile_graphattention_kernel(tc, rel, embed, src_embed, offs, out):
         embed_ones = held.tile([P, VB, PITCH], BF16, name="embed_ones")
         src_sb = held.tile([E, N], BF16, name="src_sb")
         rel_sb = [held.tile([P, S], F32, name=f"rel{b}") for b in range(VB)]
-        for b in range(TURN):
-            nc.sync.dma_start(embed_ones[:, b, 0:E], embed[b * P : (b + 1) * P, :])
-        nc.sync.dma_start(src_sb[:], src_embed)
-        nc.sync.dma_start(rel_sb[0][:], rel[0:P, :])
-        for b in range(TURN, VB):
-            nc.sync.dma_start(embed_ones[:, b, 0:E], embed[b * P : (b + 1) * P, :])
-        for b in range(1, VB):
+        def load_rel(b):
             nc.sync.dma_start(rel_sb[b][:], rel[b * P : (b + 1) * P, :])
+
+        for i, (b0, nb) in enumerate(TURNS):
+            for b in range(b0, b0 + nb):
+                nc.sync.dma_start(embed_ones[:, b, 0:E], embed[b * P : (b + 1) * P, :])
+            if i == 0:
+                nc.sync.dma_start(src_sb[:], src_embed)
+            if i < AHEAD:
+                load_rel(i)
+        for b in range(AHEAD, VB):
+            load_rel(b)
         nc.gpsimd.memset(embed_ones[:, :, E:W], 1.0)
 
         warm = held.tile([P, 2], F32, name="warm")
@@ -84,11 +88,11 @@ def tile_graphattention_kernel(tc, rel, embed, src_embed, offs, out):
             nc.scalar.activation(expo[b][:], base_ps[:], ACT.Exp)
 
 
-        embT_ps = sums_ps.tile([E, TURN * P], BF16, name="embT_ps", tag="bank")
-        for b0 in range(0, VB, TURN):
-            for k in range(TURN):
+        embT_ps = sums_ps.tile([E, 4 * P], BF16, name="embT_ps", tag="bank")
+        for b0, nb in TURNS:
+            for k in range(nb):
                 nc.tensor.transpose(embT_ps[:, k * P : (k + 1) * P], embed_ones[:, b0 + k, 0:E], ident[:])
-            nc.vector.tensor_copy(embT[:, b0 * P : (b0 + TURN) * P], embT_ps[:])
+            nc.vector.tensor_copy(embT[:, b0 * P : (b0 + nb) * P], embT_ps[:, 0 : nb * P])
             if b0 == 0:
                 for b in range(AHEAD):
                     start_block(b)

import concourse.mybir as mybir
from concourse.masks import make_identity

V, S, E, R, N = 1024, 1024, 128, 8, 512
P = 128
VB = V // P
JC = N // P
FLOPS = 2 * V * E * N * (R + 1)
AHEAD = 2
W = E + 2
PITCH = 144
TURNS = ((0, 2), (2, 2), (4, 4))
FIRST = 3
LATER = (3, 4, 7, 5, 6)
LAST = LATER[-1]
BANKS = ((0, 2), (2, 2))
LAST_BANKS = ((0, 2), (2, 1), (3, 1))
LAST_GROUPS = (4, 8, 4)
GROUP = 2

F32 = mybir.dt.float32
BF16 = mybir.dt.bfloat16
U16 = mybir.dt.uint16
ACT = mybir.ActivationFunctionType
ALU = mybir.AluOpType


def tile_graphattention_kernel(tc, rel, embed, src_embed, offs, out):
    nc = tc.nc
    with (
        tc.tile_pool(name="held", bufs=1) as held,
        tc.tile_pool(name="qpool", bufs=8) as qpool,
        tc.tile_pool(name="maskpool", bufs=3) as maskpool,
        tc.tile_pool(name="work", bufs=4) as work,
        tc.psum_pool(name="setup_ps", bufs=AHEAD) as setup_ps,
        tc.psum_pool(name="sums_ps", bufs=2 * FIRST) as sums_ps,
    ):
        offsets = held.tile([P, N // 16], U16, name="offsets")
        nc.sync.dma_start(offsets[:], offs)
        embed_ones = held.tile([P, VB, PITCH], BF16, name="embed_ones")
        src_sb = held.tile([E, N], BF16, name="src_sb")
        rel_sb = [held.tile([P, S], F32, name=f"rel{b}") for b in range(VB)]
        def load_rel(b):
            nc.sync.dma_start(rel_sb[b][:], rel[b * P : (b + 1) * P, :])

        for i, (b0, nb) in enumerate(TURNS):
            for b in range(b0, b0 + nb):
                nc.sync.dma_start(embed_ones[:, b, 0:E], embed[b * P : (b + 1) * P, :])
            if i == 0:
                nc.sync.dma_start(src_sb[:], src_embed)
            if i < AHEAD:
                load_rel(i)
        for b in range(AHEAD, VB):
            load_rel(b)
        nc.gpsimd.memset(embed_ones[:, :, E:W], 1.0)

        warm = held.tile([P, 2], F32, name="warm")
        nc.vector.memset(warm[:, 0:1], 1.0)
        nc.scalar.activation(warm[:, 1:2], warm[:, 0:1], ACT.Exp)

        ident = held.tile([P, P], BF16, name="ident")
        make_identity(nc, ident[:])
        ident_f32 = held.tile([P, P], F32, name="ident_f32")
        make_identity(nc, ident_f32[:])
        less_seven = held.tile([P, 1], F32, name="less_seven")
        nc.gpsimd.memset(less_seven[:], -float(R - 1))

        looked_up = {}
        picked = held.tile([P, VB, N], BF16, name="picked")
        expo = {}
        gain = held.tile([P, VB, N], BF16, name="gain")
        embT = held.tile([E, V], BF16, name="embT")
        eighth = held.tile([P, P], BF16, name="eighth")
        sum_row = held.tile([P, W], BF16, name="sum_row")
        relu_mask = held.tile([P, VB // 2, N], BF16, name="relu_mask")
        quot = held.tile([P, R, JC, E], F32, name="quot")
        finished = []
        mask_of = {}
        place = {}

        def start_block(b):
            base_ps = setup_ps.tile([P, N], F32, name="base_ps", tag="setup")
            nc.tensor.matmul(base_ps[:], embT[:, b * P : (b + 1) * P], src_sb[:], start=True, stop=True)
            looked_up[b] = work.tile([P, N], F32, name="looked_up")
            nc.vector.tensor_copy(looked_up[b][:, 0:1], embT[:, 0:1])
            nc.scalar.activation(looked_up[b][:], rel_sb[b][:].indirect(offsets[:]), ACT.Copy)
            expo[b] = work.tile([P, N], BF16, name="expo")
            nc.scalar.activation(expo[b][:], base_ps[:], ACT.Exp)


        embT_ps = sums_ps.tile([E, 4 * P], BF16, name="embT_ps", tag="bank")
        for b0, nb in TURNS:
            for k in range(nb):
                nc.tensor.transpose(embT_ps[:, k * P : (k + 1) * P], embed_ones[:, b0 + k, 0:E], ident[:])
            nc.vector.tensor_copy(embT[:, b0 * P : (b0 + nb) * P], embT_ps[:, 0 : nb * P])
            if b0 == 0:
                for b in range(AHEAD):
                    start_block(b)

        nc.vector.tensor_scalar(eighth[:], embT[:, V - P : V], 0.0, 0.125, op0=ALU.mult, op1=ALU.add)
        colsum_ps = sums_ps.tile([P, W], F32, name="colsum_ps", tag="bank")
        for b in range(VB):
            nc.tensor.matmul(colsum_ps[:], eighth[:], embed_ones[:, b, 0:W], start=(b == 0), stop=(b == VB - 1))
        nc.vector.tensor_copy(sum_row[:], colsum_ps[:])
        rest = slice(P // 2, P)
        nc.vector.tensor_sub(sum_row[rest, :], colsum_ps[rest, :], sum_row[rest, :])

        def banks_in(r, c0, n):
            return [(c, m) for c, m in (LAST_BANKS if r == LAST else BANKS) if c0 <= c and c + m <= c0 + n]

        def open_bank(r, c0, n):
            if r == LATER[0]:
                bank = setup_ps.tile([P, n, W], F32, name="late_bank", tag="setup")
            else:
                bank = sums_ps.tile([P, n, W], F32, name="bank", tag="bank")
            row_of_each_chunk = sum_row[:].unsqueeze(1).to_broadcast([P, n, W])
            nc.tensor.matmul(bank[:], eighth[:], row_of_each_chunk, start=True, stop=False)
            for i in range(n):
                place[r, c0 + i] = bank, i

        def finish_block(b):
            if b + AHEAD < VB:
                start_block(b + AHEAD)
            if b < VB - 1:
                nc.vector.tensor_copy(picked[:, b, :], looked_up[b][:])
            else:
                nc.scalar.copy(picked[:, b, :], looked_up[b][:])
            nc.vector.tensor_scalar(gain[:, b, :], expo[b][:], -1.0, 3.0e38, op0=ALU.add, op1=ALU.min)
            finished.append(b)
            if b == VB - 1:
                nc.scalar.activation(relu_mask[:], picked[:, VB // 2 : VB, :], ACT.Relu, bias=less_seven[:])


        def make_masks(r0, nr, b0, nb, c0, n):
            for b in range(b0, b0 + nb):
                if b not in finished:
                    finish_block(b)
            tokens = slice(c0 * P, (c0 + n) * P)
            if r0 == R - 1 and b0 >= VB // 2:
                mask_of[r0, b0, c0] = relu_mask[:, b0 - VB // 2 : b0 - VB // 2 + nb, tokens]
                return
            mask = maskpool.tile([P, nr * nb, n * P], BF16, name="mask")
            for i in range(nr):
                nc.vector.tensor_single_scalar(
                    mask[:, i * nb : (i + 1) * nb, :], picked[:, b0 : b0 + nb, tokens], float(r0 + i + 1), op=ALU.is_equal
                )
            mask_of[r0, b0, c0] = mask[:]

        def add_step(r0, nr, b0, nb, c0, n):
            q = qpool.tile([P, nr * nb, n * P], BF16, name="q")
            factor = gain[:, b0 : b0 + nb, c0 * P : (c0 + n) * P]
            if nr > 1:
                factor = factor.to_broadcast([P, nr, n * P])
            nc.vector.tensor_mul(q[:], mask_of[r0, b0, c0], factor)
            for i in range(nr):
                for k in range(nb):
                    for c in range(c0, c0 + n):
                        bank, slot = place[r0 + i, c]
                        nc.tensor.matmul(
                            bank[:, slot, :],
                            q[:, i * nb + k, (c - c0) * P : (c - c0 + 1) * P],
                            embed_ones[:, b0 + k, 0:W],
                            start=False,
                            stop=(b0 + k == VB - 1 and slot == bank.shape[1] - 1),
                        )

        def divide(r, c0, n):
            bank, _ = place[r, c0]
            recip = work.tile([P, n, 1], F32, name="recip")
            if r == LAST and c0 + n == JC:
                nc.vector.reciprocal(recip[:], bank[:, :, E : E + 1])
                nc.vector.tensor_mul(quot[:, r, c0 : c0 + n, :], bank[:, :, 0:E], recip[:].to_broadcast([P, n, E]))
                return
            rsqrt = work.tile([P, n, 1], F32, name="rsqrt")
            nc.scalar.activation(rsqrt[:], bank[:, :, E : E + 1], ACT.Abs_reciprocal_sqrt)
            nc.scalar.activation(recip[:], rsqrt[:], ACT.Square)
            for i in range(n):
                nc.scalar.activation(quot[:, r, c0 + i, :], bank[:, i, 0:E], ACT.Identity, scale=recip[:, i, :])

        def turn_back(r, c0, n):
            out_ps = sums_ps.tile([E, n * P], F32, name="out_ps", tag="bank")
            for i in range(n):
                nc.tensor.transpose(out_ps[:, i * P : (i + 1) * P], quot[:, r, c0 + i, :], ident_f32[:])
            res = work.tile([E, n * P], F32, name="res")
            if r == LAST and c0 + n == JC:
                nc.vector.tensor_copy(res[:], out_ps[:])
            else:
                nc.scalar.copy(res[:], out_ps[:])
            nc.sync.dma_start(out[r * E : (r + 1) * E, c0 * P : (c0 + n) * P], res[:])

        steps = [(0, FIRST, b, 1, 0, JC) for b in range(VB)]
        steps += [(r, 1, b0, GROUP, 0, JC) for r in LATER[:-1] for b0 in range(0, VB, GROUP)]
        steps += [
            (LAST, 1, b0, group, c0, n) for (c0, n), group in zip(LAST_BANKS, LAST_GROUPS) for b0 in range(0, VB, group)
        ]
        divided = []
        make_masks(*steps[0])
        for s, (r0, nr, b0, nb, c0, n) in enumerate(steps):
            if s + 1 < len(steps):
                make_masks(*steps[s + 1])
            for r in range(r0, r0 + nr):
                if b0 == 0:
                    for bank in banks_in(r, c0, n):
                        open_bank(r, *bank)
            add_step(r0, nr, b0, nb, c0, n)
            if s > VB + AHEAD and s % 2 == 1 and divided and r0 != LAST:
                turn_back(*divided.pop(0))
            if b0 + nb == VB:
                for r in range(r0, r0 + nr):
                    for bank in banks_in(r, c0, n):
                        divide(r, *bank)
                    divided.append((r, c0, n))
        for part in divided:
            turn_back(*part)
